import numpy as np
import ml_dtypes


def mxq(x, axis, fmt="e4m3"):
    dtype, down = {"e4m3": (ml_dtypes.float8_e4m3fn, 7), "e5m2": (ml_dtypes.float8_e5m2, 14)}[fmt]
    v = np.moveaxis(np.asarray(x, np.float32).astype(ml_dtypes.bfloat16).astype(np.float64), axis, -1)
    blocks = v.reshape(v.shape[:-1] + (-1, 32))
    amax = np.abs(blocks).max(-1, keepdims=True)
    byte = np.maximum(np.where(amax > 0, np.frexp(amax)[1] - 1 + 127, 0) - down, 1)
    scale = np.exp2(byte - 127.0)
    codes = (blocks / scale).astype(np.float32).astype(dtype).astype(np.float64)
    return np.moveaxis((codes * scale).reshape(v.shape), -1, axis)


WIDE = False


def mx_kscale(k):
    if not WIDE:
        return np.ones(k)
    levels = np.array([10, -10, 5, -5, 0])
    a = np.random.permutation(np.resize(levels, k // 512 * 4)).reshape(k // 512, 4)
    idx = np.arange(k)
    return np.exp2(a[idx // 512, idx % 128 // 32])


BF16 = ml_dtypes.bfloat16


def bf(x):
    return np.asarray(x, np.float32).astype(BF16)


def f64(x):
    return np.asarray(x).astype(np.float64)


B, S, E, R = 1, 512, 1024, 4
F = R * E
EPS = 1e-5


def layer_norm(y, g, b):
    mu = y.mean(-1, keepdims=True)
    var = np.square(y - mu).mean(-1, keepdims=True)
    return (y - mu) / np.sqrt(var + EPS) * g + b


def setup_inputs():
    t = mx_kscale(F)
    return {"x2": bf(np.random.standard_normal((B, S, E))),
            "mlp_w1": bf(np.random.standard_normal((E, F)) / np.sqrt(E) * t),
            "mlp_b1": bf(np.random.standard_normal(F) * 0.3 * t),
            "mlp_w2": bf(np.random.standard_normal((F, E)) * 1.5 / np.sqrt(F) / t[:, None]),
            "mlp_b2": bf(np.random.standard_normal(E) * 0.3),
            "ln3_g": bf(1.0 + 0.1 * np.random.standard_normal(E)),
            "ln3_b": bf(0.2 * np.random.standard_normal(E))}


def reference(x2, mlp_w1, mlp_b1, mlp_w2, mlp_b2, ln3_g, ln3_b):
    xf = f64(x2)
    h = np.maximum((mxq(xf, 2, "e4m3") @ mxq(f64(mlp_w1), 0, "e4m3")) + f64(mlp_b1), 0.0)
    m = np.maximum((mxq(h, 2, "e4m3") @ mxq(f64(mlp_w2), 0, "e4m3")) + f64(mlp_b2), 0.0)
    return layer_norm(xf + m, f64(ln3_g), f64(ln3_b))

@@ -1,0 +1,295 @@
+from contextlib import ExitStack
+
+import concourse.mybir as mybir
+from concourse.masks import make_identity
+
+FP8X4 = mybir.dt.float8_e4m3fn_x4
+BF16 = mybir.dt.bfloat16
+F32 = mybir.dt.float32
+U32 = mybir.dt.uint32
+U8 = mybir.dt.uint8
+ACT = mybir.ActivationFunctionType
+ALU = mybir.AluOpType
+
+P = 128
+PACK = 4
+K_PASS = P * PACK
+N_TILE = 512
+RUN = 4
+
+TOKENS = 512
+E = 1024
+F = 4096
+EPS = 1e-5
+
+TOKEN_TILES = TOKENS // P
+E_PASSES = E // K_PASS
+F_PASSES = F // K_PASS
+E_HALVES = E // N_TILE
+W1_LOAD_COLS = 1024
+
+FLOPS = 2 * TOKENS * E * F * 2
+
+
+def tile_transformerdecoderblock_pb_kernel(
+    tc, x2, mlp_w1, mlp_b1, mlp_w2, mlp_b2, ln3_g, ln3_b, out
+):
+    nc = tc.nc
+    x_rows = x2.flatten_outer_dims().rearrange("(r i) e -> r i e", i=TOKEN_TILES)
+    out_rows = out.flatten_outer_dims().rearrange("(r i) e -> r i e", i=TOKEN_TILES)
+
+    with ExitStack() as ctx:
+        keep = ctx.enter_context(tc.tile_pool(name="keep", bufs=1))
+        stage = ctx.enter_context(tc.tile_pool(name="stage", bufs=4))
+        psum = ctx.enter_context(tc.psum_pool(name="psum", bufs=8))
+
+        def regroup_on_both(rows):
+            grouped = stage.tile([P, N_TILE, PACK], BF16, align_bytes=64, bufs=6)
+            dst = grouped[:].rearrange("p (c i) t -> p c t i", i=RUN)
+            src = rows.rearrange("p t (c i) -> p c t i", i=RUN)
+            cut = N_TILE // RUN // 2
+            nc.vector.tensor_copy(out=dst[:, :cut], in_=src[:, :cut])
+            nc.scalar.copy(out=dst[:, cut:], in_=src[:, cut:])
+            return grouped
+
+        def regroup_on_vector(rows):
+            grouped = stage.tile([P, N_TILE, PACK], BF16, align_bytes=64, bufs=6)
+            nc.vector.tensor_copy(
+                out=grouped[:].rearrange("p (c i) t -> p c t i", i=RUN),
+                in_=rows.rearrange("p t (c i) -> p c t i", i=RUN),
+            )
+            return grouped
+
+        def quantise(grouped, words, scales):
+            nc.vector.quantize_mx(
+                out=words.bitcast(FP8X4),
+                scales=scales,
+                in_=grouped[:].rearrange("p c t -> p (c t)"),
+            )
+
+        ident_f32 = keep.tile([P, P], F32)
+        make_identity(nc, ident_f32[:])
+        ident_bf16 = keep.tile([P, P], BF16)
+        make_identity(nc, ident_bf16[:])
+        one = keep.tile([P, 1], F32)
+        nc.vector.memset(one[:], 1.0)
+        warm = keep.tile([P, 1], F32)
+        nc.scalar.activation(out=warm[:], in_=one[:], func=ACT.Sqrt)
+
+        x_sb = keep.tile([P, TOKEN_TILES, E], BF16)
+        nc.sync.dma_start(out=x_sb[:], in_=x_rows)
+        b1_rows = keep.tile([P, P], BF16)
+        nc.vector.memset(b1_rows[:], 0.0)
+        nc.sync.dma_start(
+            out=b1_rows[: F // P, :], in_=mlp_b1.rearrange("(r c) -> r c", c=P)
+        )
+
+        w2_raw = []
+        for fp in range(F_PASSES):
+            w2_rows = keep.tile([P, PACK, E], BF16, name="w2_raw%d" % fp)
+            w2_raw.append(w2_rows)
+        b2_all = keep.tile([P, E], BF16)
+        g_all = keep.tile([P, E], BF16)
+        b_all = keep.tile([P, E], BF16)
+
+        x_words = keep.tile([P, E_PASSES, TOKENS], U32, align_bytes=64)
+        x_scales = keep.tile([P, E_PASSES, TOKENS], U8, align_bytes=64)
+        h_words = keep.tile([P, F_PASSES, TOKENS], U32, align_bytes=64)
+        h_scales = keep.tile([P, F_PASSES, TOKENS], U8, align_bytes=64)
+        b1_sb = keep.tile([P, F // P], F32)
+
+        with tc.tile_pool(name="w1", bufs=1) as w1_pool:
+            w1_raw = {}
+            for lc in range(F // W1_LOAD_COLS):
+                for ep in range(E_PASSES):
+                    w1_rows = w1_pool.tile(
+                        [P, PACK, W1_LOAD_COLS], BF16, name="w1_raw%d_%d" % (ep, lc)
+                    )
+                    nc.sync.dma_start(
+                        out=w1_rows[:],
+                        in_=mlp_w1[
+                            ep * K_PASS : (ep + 1) * K_PASS,
+                            lc * W1_LOAD_COLS : (lc + 1) * W1_LOAD_COLS,
+                        ].rearrange("(p j) w -> p j w", j=PACK),
+                    )
+                    w1_raw[(ep, lc)] = w1_rows
+            for fp in range(F_PASSES):
+                nc.sync.dma_start(
+                    out=w2_raw[fp][:],
+                    in_=mlp_w2[fp * K_PASS : (fp + 1) * K_PASS, :].rearrange(
+                        "(t p) e -> p t e", p=P
+                    ),
+                )
+            nc.sync.dma_start(out=b2_all[:], in_=mlp_b2.partition_broadcast(P))
+            nc.sync.dma_start(out=g_all[:], in_=ln3_g.partition_broadcast(P))
+            nc.sync.dma_start(out=b_all[:], in_=ln3_b.partition_broadcast(P))
+
+            x_pairs = x_sb[:].bitcast(F32)
+            words_per_pass = K_PASS // 2
+            for ep in range(E_PASSES):
+                x_grouped = stage.tile([P, N_TILE, PACK], BF16, align_bytes=64, bufs=6, tag="grouped")
+                x_grouped_pairs = x_grouped[:].bitcast(F32)
+                for pair in range(TOKEN_TILES // 2):
+                    xt = psum.tile([P, 2, 2 * P], F32, tag="bank")
+                    for u in range(2):
+                        for j in range(2):
+                            nc.tensor.transpose(
+                                out=xt[:, u, j * P : (j + 1) * P],
+                                in_=x_pairs[
+                                    :,
+                                    2 * pair + j,
+                                    ep * words_per_pass + u : (ep + 1) * words_per_pass : 2,
+                                ],
+                                identity=ident_f32[:],
+                            )
+                    dst = x_grouped_pairs[:, pair * 2 * P : (pair + 1) * 2 * P, :]
+                    src = xt[:].rearrange("p u c -> p c u")
+                    if pair == 0:
+                        nc.vector.tensor_copy(out=dst, in_=src)
+                    else:
+                        nc.scalar.copy(out=dst, in_=src)
+                quantise(x_grouped, x_words[:, ep, :], x_scales[:, ep, :])
+
+            b1_t = psum.tile([P, P], BF16, tag="bank")
+            nc.tensor.transpose(out=b1_t[:], in_=b1_rows[:], identity=ident_bf16[:])
+            nc.vector.tensor_copy(out=b1_sb[:], in_=b1_t[:, : F // P])
+
+            w1_grouped = {}
+            h_acc = {}
+            h_rows = {}
+            for s in range(F_PASSES + 2):
+                if s < F_PASSES:
+                    for ep in range(E_PASSES):
+                        lc, part = divmod(s * N_TILE, W1_LOAD_COLS)
+                        w1_grouped[ep] = regroup_on_both(
+                            w1_raw[(ep, lc)][:, :, part : part + N_TILE]
+                        )
+                if s >= 2:
+                    h_grouped = regroup_on_vector(h_rows[s - 2][:])
+                if s < F_PASSES:
+                    w1_words = stage.tile([P, E_PASSES, N_TILE], U32, align_bytes=64, bufs=2)
+                    w1_scales = stage.tile([P, E_PASSES, N_TILE], U8, align_bytes=64, bufs=2)
+                    for ep in range(E_PASSES):
+                        quantise(w1_grouped[ep], w1_words[:, ep, :], w1_scales[:, ep, :])
+                if s >= 2:
+                    quantise(h_grouped, h_words[:, s - 2, :], h_scales[:, s - 2, :])
+                if s < F_PASSES:
+                    h_acc[s] = []
+                    for t in range(PACK):
+                        acc = psum.tile([P, N_TILE], F32, tag="bank")
+                        for ep in range(E_PASSES):
+                            nc.tensor.matmul_mx(
+                                out=acc[:],
+                                lhsT=w1_words[:, ep, t * P : (t + 1) * P].bitcast(FP8X4),
+                                lhsT_scale=w1_scales[:, ep, t * P : (t + 1) * P],
+                                rhs=x_words[:, ep, :].bitcast(FP8X4),
+                                rhs_scale=x_scales[:, ep, :],
+                                start=(ep == 0),
+                                stop=(ep == E_PASSES - 1),
+                            )
+                        h_acc[s].append(acc)
+                if 1 <= s <= F_PASSES:
+                    h_t = stage.tile([P, PACK, TOKENS], BF16, bufs=3)
+                    for t in range(PACK):
+                        col = (s - 1) * PACK + t
+                        nc.scalar.activation(
+                            out=h_t[:, t, :],
+                            in_=h_acc[s - 1][t][:],
+                            func=ACT.Relu,
+                            bias=b1_sb[:, col : col + 1],
+                        )
+                    h_rows[s - 1] = h_t
+
+        tail = ctx.enter_context(tc.tile_pool(name="tail", bufs=2))
+        y = tail.tile([P, TOKEN_TILES, E], F32, bufs=1)
+        y_sum = tail.tile([P, TOKEN_TILES, E_HALVES], F32, bufs=1)
+        neg_mean = tail.tile([P, TOKEN_TILES], F32, bufs=1)
+        sq_sum = tail.tile([P, TOKEN_TILES], F32, bufs=1)
+        std = tail.tile([P, TOKEN_TILES], F32, bufs=1)
+        rstd = tail.tile([P, TOKEN_TILES], F32, bufs=1)
+
+        chunks = [(eh, fp) for eh in range(E_HALVES) for fp in range(F_PASSES)]
+        w2_grouped = {}
+        m_acc = {}
+        for c in range(len(chunks) + 1):
+            if c < len(chunks):
+                eh, fp = chunks[c]
+                w2_grouped[c] = regroup_on_both(
+                    w2_raw[fp][:, :, eh * N_TILE : (eh + 1) * N_TILE]
+                )
+            if c >= 1:
+                eh, fp = chunks[c - 1]
+                w2_words = stage.tile([P, N_TILE], U32, align_bytes=64, bufs=3)
+                w2_scales = stage.tile([P, N_TILE], U8, align_bytes=64, bufs=3)
+                quantise(w2_grouped[c - 1], w2_words[:], w2_scales[:])
+                for i in range(TOKEN_TILES):
+                    if fp == 0:
+                        acc = psum.tile([P, N_TILE], F32, tag="bank")
+                        m_acc[i] = acc
+                    nc.tensor.matmul_mx(
+                        out=m_acc[i][:],
+                        lhsT=h_words[:, fp, i * P : (i + 1) * P].bitcast(FP8X4),
+                        lhsT_scale=h_scales[:, fp, i * P : (i + 1) * P],
+                        rhs=w2_words[:].bitcast(FP8X4),
+                        rhs_scale=w2_scales[:],
+                        start=(fp == 0),
+                        stop=(fp == F_PASSES - 1),
+                    )
+                if fp == F_PASSES - 1:
+                    cols = slice(eh * N_TILE, (eh + 1) * N_TILE)
+                    for i in range(TOKEN_TILES):
+                        z = tail.tile([P, N_TILE], F32)
+                        nc.vector.tensor_tensor(
+                            out=z[:], in0=m_acc[i][:], in1=b2_all[:, cols], op=ALU.add
+                        )
+                        nc.vector.scalar_tensor_tensor(
+                            out=y[:, i, cols],
+                            in0=z[:],
+                            scalar=0.0,
+                            in1=x_sb[:, i, cols],
+                            op0=ALU.max,
+                            op1=ALU.add,
+                            accum_out=y_sum[:, i, eh : eh + 1],
+                        )
+
+        for i in range(TOKEN_TILES):
+            one_tile = slice(i, i + 1)
+            nc.vector.tensor_scalar(
+                out=neg_mean[:, one_tile],
+                in0=y_sum[:, i, 0:1],
+                scalar1=y_sum[:, i, 1:2],
+                scalar2=-1.0 / E,
+                op0=ALU.add,
+                op1=ALU.mult,
+            )
+            squares = tail.tile([P, E], BF16, bufs=4)
+            nc.scalar.activation(
+                out=squares[:],
+                in_=y[:, i, :],
+                func=ACT.Square,
+                bias=neg_mean[:, one_tile],
+                accum_out=sq_sum[:, one_tile],
+            )
+            nc.scalar.activation(
+                out=std[:, one_tile], in_=sq_sum[:, one_tile], func=ACT.Sqrt, scale=1.0 / E, bias=EPS
+            )
+            centred = tail.tile([P, E], F32)
+            nc.vector.scalar_tensor_tensor(
+                out=centred[:],
+                in0=y[:, i, :],
+                scalar=neg_mean[:, one_tile],
+                in1=g_all[:],
+                op0=ALU.add,
+                op1=ALU.mult,
+            )
+            nc.vector.reciprocal(out=rstd[:, one_tile], in_=std[:, one_tile])
+            result = tail.tile([P, E], F32)
+            nc.vector.scalar_tensor_tensor(
+                out=result[:],
+                in0=centred[:],
+                scalar=rstd[:, one_tile],
+                in1=b_all[:],
+                op0=ALU.mult,
+                op1=ALU.add,
+            )
+            nc.sync.dma_start(out=out_rows[:, i, :], in_=result[:])

@@ -26,7 +26,12 @@ TOKEN_TILES = TOKENS // P
 E_PASSES = E // K_PASS
 F_PASSES = F // K_PASS
 E_HALVES = E // N_TILE
-W1_LOAD_COLS = 1024
+
+W1_STEPS = F // N_TILE
+W2_STEPS = E_HALVES * F_PASSES // 2
+STEPS = W1_STEPS + W2_STEPS
+W1_VECTOR_COLS = 320
+W2_VECTOR_COLS = 224
 
 FLOPS = 2 * TOKENS * E * F * 2
 
@@ -39,25 +44,19 @@ def tile_transformerdecoderblock_pb_kernel(
     out_rows = out.flatten_outer_dims().rearrange("(r i) e -> r i e", i=TOKEN_TILES)
 
     with ExitStack() as ctx:
+        ctx.enter_context(tc.manual_schedule())
         keep = ctx.enter_context(tc.tile_pool(name="keep", bufs=1))
-        stage = ctx.enter_context(tc.tile_pool(name="stage", bufs=4))
+        stage = ctx.enter_context(tc.tile_pool(name="stage", bufs=2))
         psum = ctx.enter_context(tc.psum_pool(name="psum", bufs=8))
 
-        def regroup_on_both(rows):
+        def regroup(rows, vector_cols):
             grouped = stage.tile([P, N_TILE, PACK], BF16, align_bytes=64, bufs=6)
             dst = grouped[:].rearrange("p (c i) t -> p c t i", i=RUN)
             src = rows.rearrange("p t (c i) -> p c t i", i=RUN)
-            cut = N_TILE // RUN // 2
+            cut = vector_cols // RUN
             nc.vector.tensor_copy(out=dst[:, :cut], in_=src[:, :cut])
-            nc.scalar.copy(out=dst[:, cut:], in_=src[:, cut:])
-            return grouped
-
-        def regroup_on_vector(rows):
-            grouped = stage.tile([P, N_TILE, PACK], BF16, align_bytes=64, bufs=6)
-            nc.vector.tensor_copy(
-                out=grouped[:].rearrange("p (c i) t -> p c t i", i=RUN),
-                in_=rows.rearrange("p t (c i) -> p c t i", i=RUN),
-            )
+            if vector_cols < N_TILE:
+                nc.scalar.copy(out=dst[:, cut:], in_=src[:, cut:])
             return grouped
 
         def quantise(grouped, words, scales):
@@ -77,219 +76,235 @@ def tile_transformerdecoderblock_pb_kernel(
         nc.scalar.activation(out=warm[:], in_=one[:], func=ACT.Sqrt)
 
         x_sb = keep.tile([P, TOKEN_TILES, E], BF16)
-        nc.sync.dma_start(out=x_sb[:], in_=x_rows)
         b1_rows = keep.tile([P, P], BF16)
-        nc.vector.memset(b1_rows[:], 0.0)
-        nc.sync.dma_start(
-            out=b1_rows[: F // P, :], in_=mlp_b1.rearrange("(r c) -> r c", c=P)
-        )
-
-        w2_raw = []
-        for fp in range(F_PASSES):
-            w2_rows = keep.tile([P, PACK, E], BF16, name="w2_raw%d" % fp)
-            w2_raw.append(w2_rows)
+        b1_sb = keep.tile([P, F // P], F32)
         b2_all = keep.tile([P, E], BF16)
         g_all = keep.tile([P, E], BF16)
         b_all = keep.tile([P, E], BF16)
-
         x_words = keep.tile([P, E_PASSES, TOKENS], U32, align_bytes=64)
         x_scales = keep.tile([P, E_PASSES, TOKENS], U8, align_bytes=64)
         h_words = keep.tile([P, F_PASSES, TOKENS], U32, align_bytes=64)
         h_scales = keep.tile([P, F_PASSES, TOKENS], U8, align_bytes=64)
-        b1_sb = keep.tile([P, F // P], F32)
+        w1_raw = {}
+        w2_raw = {}
+
+        def weight_chunks(s):
+            if s < W1_STEPS:
+                return [w1_raw[(s, ep)][:] for ep in range(E_PASSES)]
+            eh, pair = divmod(s - W1_STEPS, F_PASSES // 2)
+            return [w2_raw[(eh, 2 * pair + a)][:] for a in range(2)]
+
+        def regroup_weights(s):
+            vector_cols = W1_VECTOR_COLS if s < W1_STEPS else W2_VECTOR_COLS
+            return [regroup(rows, vector_cols) for rows in weight_chunks(s)]
+
+        grouped_of = {}
+        h_acc = {}
+        h_rows = {}
+        m_acc = {}
+        z_of = {}
+        late = {}
+
+        def first_matmul(s, words, scales):
+            h_acc[s] = []
+            for t in range(PACK):
+                acc = psum.tile([P, N_TILE], F32, tag="bank")
+                for ep in range(E_PASSES):
+                    nc.tensor.matmul_mx(
+                        out=acc[:],
+                        lhsT=words[:, ep, t * P : (t + 1) * P].bitcast(FP8X4),
+                        lhsT_scale=scales[:, ep, t * P : (t + 1) * P],
+                        rhs=x_words[:, ep, :].bitcast(FP8X4),
+                        rhs_scale=x_scales[:, ep, :],
+                        start=(ep == 0),
+                        stop=(ep == E_PASSES - 1),
+                    )
+                h_acc[s].append(acc)
+
+        def bias_relu(s):
+            h_t = stage.tile([P, PACK, TOKENS], BF16, bufs=3)
+            for t in range(PACK):
+                col = s * PACK + t
+                nc.scalar.activation(
+                    out=h_t[:, t, :], in_=h_acc[s][t][:], func=ACT.Relu, bias=b1_sb[:, col : col + 1]
+                )
+            h_rows[s] = h_t
+
+        def second_matmul(s, words, scales):
+            eh, pair = divmod(s - W1_STEPS, F_PASSES // 2)
+            for a in range(2):
+                fp = 2 * pair + a
+                for i in range(TOKEN_TILES):
+                    if fp == 0:
+                        acc = psum.tile([P, N_TILE], F32, tag="bank")
+                        m_acc[(eh, i)] = acc
+                    nc.tensor.matmul_mx(
+                        out=m_acc[(eh, i)][:],
+                        lhsT=h_words[:, fp, i * P : (i + 1) * P].bitcast(FP8X4),
+                        lhsT_scale=h_scales[:, fp, i * P : (i + 1) * P],
+                        rhs=words[:, a, :].bitcast(FP8X4),
+                        rhs_scale=scales[:, a, :],
+                        start=(fp == 0),
+                        stop=(fp == F_PASSES - 1),
+                    )
+
+        def add_bias(eh, i):
+            cols = slice(eh * N_TILE, (eh + 1) * N_TILE)
+            z = late["pool"].tile([P, N_TILE], F32, bufs=3)
+            nc.vector.tensor_tensor(out=z[:], in0=m_acc[(eh, i)][:], in1=b2_all[:, cols], op=ALU.add)
+            z_of[(eh, i)] = z
+
+        def relu_residual(eh, i):
+            cols = slice(eh * N_TILE, (eh + 1) * N_TILE)
+            nc.vector.scalar_tensor_tensor(
+                out=late["y"][:, i, cols],
+                in0=z_of[(eh, i)][:],
+                scalar=0.0,
+                in1=x_sb[:, i, cols],
+                op0=ALU.max,
+                op1=ALU.add,
+                accum_out=late["y_sum"][:, i, eh : eh + 1],
+            )
+
+        def step(s):
+            if s + 1 < STEPS:
+                grouped_of[s + 1] = regroup_weights(s + 1)
+            if 0 <= s - 2 < W1_STEPS:
+                h_grouped = regroup(h_rows[s - 2][:], N_TILE)
+            if s >= STEPS - TOKEN_TILES:
+                add_bias(0, s - (STEPS - TOKEN_TILES))
+            words = stage.tile([P, 2, N_TILE], U32, align_bytes=64)
+            scales = stage.tile([P, 2, N_TILE], U8, align_bytes=64)
+            for a in range(2):
+                quantise(grouped_of[s][a], words[:, a, :], scales[:, a, :])
+            if 0 <= s - 2 < W1_STEPS:
+                quantise(h_grouped, h_words[:, s - 2, :], h_scales[:, s - 2, :])
+            if s < W1_STEPS:
+                first_matmul(s, words, scales)
+            else:
+                second_matmul(s, words, scales)
+            if 0 <= s - 1 < W1_STEPS:
+                bias_relu(s - 1)
+            if s >= STEPS - TOKEN_TILES:
+                relu_residual(0, s - (STEPS - TOKEN_TILES))
 
         with tc.tile_pool(name="w1", bufs=1) as w1_pool:
-            w1_raw = {}
-            for lc in range(F // W1_LOAD_COLS):
+            for i in range(TOKEN_TILES):
+                nc.sync.dma_start(out=x_sb[:, i, :], in_=x_rows[:, i, :])
+            nc.vector.memset(b1_rows[:], 0.0)
+            nc.sync.dma_start(out=b1_rows[: F // P, :], in_=mlp_b1.rearrange("(r c) -> r c", c=P))
+            for s in range(W1_STEPS):
                 for ep in range(E_PASSES):
-                    w1_rows = w1_pool.tile(
-                        [P, PACK, W1_LOAD_COLS], BF16, name="w1_raw%d_%d" % (ep, lc)
-                    )
+                    w1_rows = w1_pool.tile([P, PACK, N_TILE], BF16, name="w1_raw%d_%d" % (s, ep))
                     nc.sync.dma_start(
                         out=w1_rows[:],
                         in_=mlp_w1[
-                            ep * K_PASS : (ep + 1) * K_PASS,
-                            lc * W1_LOAD_COLS : (lc + 1) * W1_LOAD_COLS,
+                            ep * K_PASS : (ep + 1) * K_PASS, s * N_TILE : (s + 1) * N_TILE
                         ].rearrange("(p j) w -> p j w", j=PACK),
                     )
-                    w1_raw[(ep, lc)] = w1_rows
-            for fp in range(F_PASSES):
-                nc.sync.dma_start(
-                    out=w2_raw[fp][:],
-                    in_=mlp_w2[fp * K_PASS : (fp + 1) * K_PASS, :].rearrange(
-                        "(t p) e -> p t e", p=P
-                    ),
-                )
+                    w1_raw[(s, ep)] = w1_rows
+            for eh in range(E_HALVES):
+                for fp in range(F_PASSES):
+                    w2_rows = keep.tile([P, PACK, N_TILE], BF16, name="w2_raw%d_%d" % (eh, fp))
+                    nc.sync.dma_start(
+                        out=w2_rows[:],
+                        in_=mlp_w2[
+                            fp * K_PASS : (fp + 1) * K_PASS, eh * N_TILE : (eh + 1) * N_TILE
+                        ].rearrange("(t p) e -> p t e", p=P),
+                    )
+                    w2_raw[(eh, fp)] = w2_rows
             nc.sync.dma_start(out=b2_all[:], in_=mlp_b2.partition_broadcast(P))
             nc.sync.dma_start(out=g_all[:], in_=ln3_g.partition_broadcast(P))
             nc.sync.dma_start(out=b_all[:], in_=ln3_b.partition_broadcast(P))
 
-            x_pairs = x_sb[:].bitcast(F32)
-            words_per_pass = K_PASS // 2
-            for ep in range(E_PASSES):
-                x_grouped = stage.tile([P, N_TILE, PACK], BF16, align_bytes=64, bufs=6, tag="grouped")
-                x_grouped_pairs = x_grouped[:].bitcast(F32)
-                for pair in range(TOKEN_TILES // 2):
-                    xt = psum.tile([P, 2, 2 * P], F32, tag="bank")
+            x_pairs = x_sb[:].bitcast(F32).rearrange("r i (ep p u) -> r i ep u p", ep=E_PASSES, u=2)
+            x_grouped = keep.tile([P, E_PASSES, TOKENS, PACK], BF16, align_bytes=64)
+            x_grouped_pairs = x_grouped[:].bitcast(F32)
+            for i in range(TOKEN_TILES):
+                xt = psum.tile([P, E_PASSES, 2, P], F32, tag="bank")
+                for ep in range(E_PASSES):
                     for u in range(2):
-                        for j in range(2):
-                            nc.tensor.transpose(
-                                out=xt[:, u, j * P : (j + 1) * P],
-                                in_=x_pairs[
-                                    :,
-                                    2 * pair + j,
-                                    ep * words_per_pass + u : (ep + 1) * words_per_pass : 2,
-                                ],
-                                identity=ident_f32[:],
-                            )
-                    dst = x_grouped_pairs[:, pair * 2 * P : (pair + 1) * 2 * P, :]
-                    src = xt[:].rearrange("p u c -> p c u")
-                    if pair == 0:
-                        nc.vector.tensor_copy(out=dst, in_=src)
-                    else:
-                        nc.scalar.copy(out=dst, in_=src)
-                quantise(x_grouped, x_words[:, ep, :], x_scales[:, ep, :])
+                        nc.tensor.transpose(out=xt[:, ep, u, :], in_=x_pairs[:, i, ep, u, :], identity=ident_f32[:])
+                dst = x_grouped_pairs[:, :, i * P : (i + 1) * P, :]
+                src = xt[:].rearrange("p ep u r -> p ep r u")
+                if i % 2 == 0:
+                    nc.vector.tensor_copy(out=dst, in_=src)
+                else:
+                    nc.scalar.copy(out=dst, in_=src)
 
             b1_t = psum.tile([P, P], BF16, tag="bank")
             nc.tensor.transpose(out=b1_t[:], in_=b1_rows[:], identity=ident_bf16[:])
+
+            grouped_of[0] = regroup_weights(0)
+            nc.vector.quantize_mx(
+                out=x_words[:].rearrange("p ep c -> p (ep c)").bitcast(FP8X4),
+                scales=x_scales[:].rearrange("p ep c -> p (ep c)"),
+                in_=x_grouped[:].rearrange("p ep c t -> p (ep c t)"),
+            )
             nc.vector.tensor_copy(out=b1_sb[:], in_=b1_t[:, : F // P])
 
-            w1_grouped = {}
-            h_acc = {}
-            h_rows = {}
-            for s in range(F_PASSES + 2):
-                if s < F_PASSES:
-                    for ep in range(E_PASSES):
-                        lc, part = divmod(s * N_TILE, W1_LOAD_COLS)
-                        w1_grouped[ep] = regroup_on_both(
-                            w1_raw[(ep, lc)][:, :, part : part + N_TILE]
-                        )
-                if s >= 2:
-                    h_grouped = regroup_on_vector(h_rows[s - 2][:])
-                if s < F_PASSES:
-                    w1_words = stage.tile([P, E_PASSES, N_TILE], U32, align_bytes=64, bufs=2)
-                    w1_scales = stage.tile([P, E_PASSES, N_TILE], U8, align_bytes=64, bufs=2)
-                    for ep in range(E_PASSES):
-                        quantise(w1_grouped[ep], w1_words[:, ep, :], w1_scales[:, ep, :])
-                if s >= 2:
-                    quantise(h_grouped, h_words[:, s - 2, :], h_scales[:, s - 2, :])
-                if s < F_PASSES:
-                    h_acc[s] = []
-                    for t in range(PACK):
-                        acc = psum.tile([P, N_TILE], F32, tag="bank")
-                        for ep in range(E_PASSES):
-                            nc.tensor.matmul_mx(
-                                out=acc[:],
-                                lhsT=w1_words[:, ep, t * P : (t + 1) * P].bitcast(FP8X4),
-                                lhsT_scale=w1_scales[:, ep, t * P : (t + 1) * P],
-                                rhs=x_words[:, ep, :].bitcast(FP8X4),
-                                rhs_scale=x_scales[:, ep, :],
-                                start=(ep == 0),
-                                stop=(ep == E_PASSES - 1),
-                            )
-                        h_acc[s].append(acc)
-                if 1 <= s <= F_PASSES:
-                    h_t = stage.tile([P, PACK, TOKENS], BF16, bufs=3)
-                    for t in range(PACK):
-                        col = (s - 1) * PACK + t
-                        nc.scalar.activation(
-                            out=h_t[:, t, :],
-                            in_=h_acc[s - 1][t][:],
-                            func=ACT.Relu,
-                            bias=b1_sb[:, col : col + 1],
-                        )
-                    h_rows[s - 1] = h_t
+            for s in range(W1_STEPS):
+                step(s)
 
         tail = ctx.enter_context(tc.tile_pool(name="tail", bufs=2))
+        late["pool"] = tail
         y = tail.tile([P, TOKEN_TILES, E], F32, bufs=1)
+        late["y"] = y
         y_sum = tail.tile([P, TOKEN_TILES, E_HALVES], F32, bufs=1)
+        late["y_sum"] = y_sum
         neg_mean = tail.tile([P, TOKEN_TILES], F32, bufs=1)
         sq_sum = tail.tile([P, TOKEN_TILES], F32, bufs=1)
         std = tail.tile([P, TOKEN_TILES], F32, bufs=1)
         rstd = tail.tile([P, TOKEN_TILES], F32, bufs=1)
 
-        chunks = [(eh, fp) for eh in range(E_HALVES) for fp in range(F_PASSES)]
-        w2_grouped = {}
-        m_acc = {}
-        for c in range(len(chunks) + 1):
-            if c < len(chunks):
-                eh, fp = chunks[c]
-                w2_grouped[c] = regroup_on_both(
-                    w2_raw[fp][:, :, eh * N_TILE : (eh + 1) * N_TILE]
-                )
-            if c >= 1:
-                eh, fp = chunks[c - 1]
-                w2_words = stage.tile([P, N_TILE], U32, align_bytes=64, bufs=3)
-                w2_scales = stage.tile([P, N_TILE], U8, align_bytes=64, bufs=3)
-                quantise(w2_grouped[c - 1], w2_words[:], w2_scales[:])
-                for i in range(TOKEN_TILES):
-                    if fp == 0:
-                        acc = psum.tile([P, N_TILE], F32, tag="bank")
-                        m_acc[i] = acc
-                    nc.tensor.matmul_mx(
-                        out=m_acc[i][:],
-                        lhsT=h_words[:, fp, i * P : (i + 1) * P].bitcast(FP8X4),
-                        lhsT_scale=h_scales[:, fp, i * P : (i + 1) * P],
-                        rhs=w2_words[:].bitcast(FP8X4),
-                        rhs_scale=w2_scales[:],
-                        start=(fp == 0),
-                        stop=(fp == F_PASSES - 1),
-                    )
-                if fp == F_PASSES - 1:
-                    cols = slice(eh * N_TILE, (eh + 1) * N_TILE)
-                    for i in range(TOKEN_TILES):
-                        z = tail.tile([P, N_TILE], F32)
-                        nc.vector.tensor_tensor(
-                            out=z[:], in0=m_acc[i][:], in1=b2_all[:, cols], op=ALU.add
-                        )
-                        nc.vector.scalar_tensor_tensor(
-                            out=y[:, i, cols],
-                            in0=z[:],
-                            scalar=0.0,
-                            in1=x_sb[:, i, cols],
-                            op0=ALU.max,
-                            op1=ALU.add,
-                            accum_out=y_sum[:, i, eh : eh + 1],
-                        )
+        for s in range(W1_STEPS, STEPS):
+            step(s)
 
+        for i in range(TOKEN_TILES + 2):
+            if i < TOKEN_TILES:
+                add_bias(1, i)
+            if 0 <= i - 1 < TOKEN_TILES:
+                relu_residual(1, i - 1)
+            if i >= 2:
+                j = i - 2
+                nc.vector.tensor_scalar(
+                    out=neg_mean[:, j : j + 1],
+                    in0=y_sum[:, j, 0:1],
+                    scalar1=y_sum[:, j, 1:2],
+                    scalar2=-1.0 / E,
+                    op0=ALU.add,
+                    op1=ALU.mult,
+                )
+                squares = tail.tile([P, E], BF16)
+                nc.scalar.activation(
+                    out=squares[:],
+                    in_=y[:, j, :],
+                    func=ACT.Square,
+                    bias=neg_mean[:, j : j + 1],
+                    accum_out=sq_sum[:, j : j + 1],
+                )
+        nc.scalar.activation(out=std[:], in_=sq_sum[:], func=ACT.Sqrt, scale=1.0 / E, bias=EPS)
+        normed = []
         for i in range(TOKEN_TILES):
-            one_tile = slice(i, i + 1)
-            nc.vector.tensor_scalar(
-                out=neg_mean[:, one_tile],
-                in0=y_sum[:, i, 0:1],
-                scalar1=y_sum[:, i, 1:2],
-                scalar2=-1.0 / E,
-                op0=ALU.add,
-                op1=ALU.mult,
-            )
-            squares = tail.tile([P, E], BF16, bufs=4)
-            nc.scalar.activation(
-                out=squares[:],
-                in_=y[:, i, :],
-                func=ACT.Square,
-                bias=neg_mean[:, one_tile],
-                accum_out=sq_sum[:, one_tile],
-            )
-            nc.scalar.activation(
-                out=std[:, one_tile], in_=sq_sum[:, one_tile], func=ACT.Sqrt, scale=1.0 / E, bias=EPS
-            )
-            centred = tail.tile([P, E], F32)
+            if i == TOKEN_TILES - 1:
+                nc.vector.reciprocal(out=rstd[:], in_=std[:])
+            centred = tail.tile([P, E], F32, bufs=TOKEN_TILES)
             nc.vector.scalar_tensor_tensor(
                 out=centred[:],
                 in0=y[:, i, :],
-                scalar=neg_mean[:, one_tile],
+                scalar=neg_mean[:, i : i + 1],
                 in1=g_all[:],
                 op0=ALU.add,
                 op1=ALU.mult,
             )
-            nc.vector.reciprocal(out=rstd[:, one_tile], in_=std[:, one_tile])
-            result = tail.tile([P, E], F32)
+            normed.append(centred)
+        for i in range(TOKEN_TILES):
             nc.vector.scalar_tensor_tensor(
-                out=result[:],
-                in0=centred[:],
-                scalar=rstd[:, one_tile],
+                out=normed[i][:],
+                in0=normed[i][:],
+                scalar=rstd[:, i : i + 1],
                 in1=b_all[:],
                 op0=ALU.mult,
                 op1=ALU.add,
             )
-            nc.sync.dma_start(out=out_rows[:, i, :], in_=result[:])
+            nc.sync.dma_start(out=out_rows[:, i, :], in_=normed[i][:])

@@ -15,7 +15,7 @@ P = 128
 PACK = 4
 K_PASS = P * PACK
 N_TILE = 512
-RUN = 4
+RUN = 8
 
 TOKENS = 512
 E = 1024

@@ -30,8 +30,9 @@ E_HALVES = E // N_TILE
 W1_STEPS = F // N_TILE
 W2_STEPS = E_HALVES * F_PASSES // 2
 STEPS = W1_STEPS + W2_STEPS
-W1_VECTOR_COLS = 320
+W1_VECTOR_COLS = 288
 W2_VECTOR_COLS = 224
+W2_LATE_VECTOR_COLS = 144
 
 FLOPS = 2 * TOKENS * E * F * 2
 
@@ -95,7 +96,7 @@ def tile_transformerdecoderblock_pb_kernel(
             return [w2_raw[(eh, 2 * pair + a)][:] for a in range(2)]
 
         def regroup_weights(s):
-            vector_cols = W1_VECTOR_COLS if s < W1_STEPS else W2_VECTOR_COLS
+            vector_cols = W1_VECTOR_COLS if s < W1_STEPS else W2_VECTOR_COLS if s < STEPS - TOKEN_TILES else W2_LATE_VECTOR_COLS
             return [regroup(rows, vector_cols) for rows in weight_chunks(s)]
 
         grouped_of = {}

@@ -15,6 +15,9 @@ P = 128
 PACK = 4
 K_PASS = P * PACK
 N_TILE = 512
+IL_STEPS = (1, 3, 5, 7)
+IL_COLS = 256
+IL_VECTOR_COLS = 448
 RUN = 8
 
 TOKENS = 512
@@ -30,9 +33,9 @@ E_HALVES = E // N_TILE
 W1_STEPS = F // N_TILE
 W2_STEPS = E_HALVES * F_PASSES // 2
 STEPS = W1_STEPS + W2_STEPS
-W1_VECTOR_COLS = 288
-W2_VECTOR_COLS = 224
-W2_LATE_VECTOR_COLS = 144
+W1_VECTOR_COLS = 304
+W2_VECTOR_COLS = 240
+W2_LATE_VECTOR_COLS = 160
 
 FLOPS = 2 * TOKENS * E * F * 2
 
@@ -48,7 +51,7 @@ def tile_transformerdecoderblock_pb_kernel(
         ctx.enter_context(tc.manual_schedule())
         keep = ctx.enter_context(tc.tile_pool(name="keep", bufs=1))
         stage = ctx.enter_context(tc.tile_pool(name="stage", bufs=2))
-        psum = ctx.enter_context(tc.psum_pool(name="psum", bufs=8))
+        psum = ctx.enter_context(tc.psum_pool(name="psum", bufs=6))
 
         def regroup(rows, vector_cols):
             grouped = stage.tile([P, N_TILE, PACK], BF16, align_bytes=64, bufs=6)
@@ -95,10 +98,33 @@ def tile_transformerdecoderblock_pb_kernel(
             eh, pair = divmod(s - W1_STEPS, F_PASSES // 2)
             return [w2_raw[(eh, 2 * pair + a)][:] for a in range(2)]
 
+        def interleave_on_tensor(s):
+            rows = weight_chunks(s)[1]
+            banks_of[s] = []
+            for c in range(0, N_TILE, IL_COLS):
+                bank = psum.tile([P, IL_COLS, PACK], BF16, tag="il", bufs=2)
+                for n in range(0, IL_COLS, P):
+                    nc.tensor.matmul(
+                        out=bank[:, n : n + P, :].rearrange("p (c i) t -> p c t i", i=RUN),
+                        lhsT=ident_bf16[:],
+                        rhs=rows[:, :, c + n : c + n + P].rearrange("p t (c i) -> p c t i", i=RUN),
+                        start=True,
+                        stop=True,
+                    )
+                banks_of[s].append(bank)
+
         def regroup_weights(s):
             vector_cols = W1_VECTOR_COLS if s < W1_STEPS else W2_VECTOR_COLS if s < STEPS - TOKEN_TILES else W2_LATE_VECTOR_COLS
-            return [regroup(rows, vector_cols) for rows in weight_chunks(s)]
+            chunks = weight_chunks(s)
+            if s not in IL_STEPS:
+                return [regroup(rows, vector_cols) for rows in chunks]
+            first = regroup(chunks[0], IL_VECTOR_COLS)
+            second = stage.tile([P, N_TILE, PACK], BF16, align_bytes=64, bufs=6, tag="grouped")
+            for half, bank in enumerate(banks_of[s]):
+                nc.scalar.copy(out=second[:, half * IL_COLS : (half + 1) * IL_COLS, :], in_=bank[:])
+            return [first, second]
 
+        banks_of = {}
         grouped_of = {}
         h_acc = {}
         h_rows = {}
@@ -137,7 +163,7 @@ def tile_transformerdecoderblock_pb_kernel(
                 fp = 2 * pair + a
                 for i in range(TOKEN_TILES):
                     if fp == 0:
-                        acc = psum.tile([P, N_TILE], F32, tag="bank")
+                        acc = psum.tile([P, N_TILE], F32, tag="il" if eh == 1 and i >= 2 else "bank", bufs=2 if eh == 1 and i >= 2 else 6)
                         m_acc[(eh, i)] = acc
                     nc.tensor.matmul_mx(
                         out=m_acc[(eh, i)][:],
@@ -168,6 +194,10 @@ def tile_transformerdecoderblock_pb_kernel(
             )
 
         def step(s):
+            if s + 1 in IL_STEPS:
+                interleave_on_tensor(s + 1)
+            if 0 <= s - 1 < W1_STEPS:
+                bias_relu(s - 1)
             if s + 1 < STEPS:
                 grouped_of[s + 1] = regroup_weights(s + 1)
             if 0 <= s - 2 < W1_STEPS:
@@ -184,8 +214,6 @@ def tile_transformerdecoderblock_pb_kernel(
                 first_matmul(s, words, scales)
             else:
                 second_matmul(s, words, scales)
-            if 0 <= s - 1 < W1_STEPS:
-                bias_relu(s - 1)
             if s >= STEPS - TOKEN_TILES:
                 relu_residual(0, s - (STEPS - TOKEN_TILES))
 

@@ -105,9 +105,9 @@ def tile_transformerdecoderblock_pb_kernel(
                 bank = psum.tile([P, IL_COLS, PACK], BF16, tag="il", bufs=2)
                 for n in range(0, IL_COLS, P):
                     nc.tensor.matmul(
-                        out=bank[:, n : n + P, :].rearrange("p (c i) t -> p c t i", i=RUN),
+                        out=bank[:, n : n + P, :].rearrange("p n t -> p t n"),
                         lhsT=ident_bf16[:],
-                        rhs=rows[:, :, c + n : c + n + P].rearrange("p t (c i) -> p c t i", i=RUN),
+                        rhs=rows[:, :, c + n : c + n + P],
                         start=True,
                         stop=True,
                     )

from contextlib import ExitStack

import concourse.mybir as mybir
from concourse.masks import make_identity

FP8X4 = mybir.dt.float8_e4m3fn_x4
BF16 = mybir.dt.bfloat16
F32 = mybir.dt.float32
U32 = mybir.dt.uint32
U8 = mybir.dt.uint8
ACT = mybir.ActivationFunctionType
ALU = mybir.AluOpType

P = 128
PACK = 4
K_PASS = P * PACK
N_TILE = 512
IL_STEPS = (1, 3, 5, 7)
IL_COLS = 256
IL_VECTOR_COLS = 448
RUN = 8

TOKENS = 512
E = 1024
F = 4096
EPS = 1e-5

TOKEN_TILES = TOKENS // P
E_PASSES = E // K_PASS
F_PASSES = F // K_PASS
E_HALVES = E // N_TILE

W1_STEPS = F // N_TILE
W2_STEPS = E_HALVES * F_PASSES // 2
STEPS = W1_STEPS + W2_STEPS
W1_VECTOR_COLS = 304
W2_VECTOR_COLS = 240
W2_LATE_VECTOR_COLS = 160

FLOPS = 2 * TOKENS * E * F * 2


def tile_transformerdecoderblock_pb_kernel(
    tc, x2, mlp_w1, mlp_b1, mlp_w2, mlp_b2, ln3_g, ln3_b, out
):
    nc = tc.nc
    x_rows = x2.flatten_outer_dims().rearrange("(r i) e -> r i e", i=TOKEN_TILES)
    out_rows = out.flatten_outer_dims().rearrange("(r i) e -> r i e", i=TOKEN_TILES)

    with ExitStack() as ctx:
        ctx.enter_context(tc.manual_schedule())
        keep = ctx.enter_context(tc.tile_pool(name="keep", bufs=1))
        stage = ctx.enter_context(tc.tile_pool(name="stage", bufs=2))
        psum = ctx.enter_context(tc.psum_pool(name="psum", bufs=6))

        def regroup(rows, vector_cols):
            grouped = stage.tile([P, N_TILE, PACK], BF16, align_bytes=64, bufs=6)
            dst = grouped[:].rearrange("p (c i) t -> p c t i", i=RUN)
            src = rows.rearrange("p t (c i) -> p c t i", i=RUN)
            cut = vector_cols // RUN
            nc.vector.tensor_copy(out=dst[:, :cut], in_=src[:, :cut])
            if vector_cols < N_TILE:
                nc.scalar.copy(out=dst[:, cut:], in_=src[:, cut:])
            return grouped

        def quantise(grouped, words, scales):
            nc.vector.quantize_mx(
                out=words.bitcast(FP8X4),
                scales=scales,
                in_=grouped[:].rearrange("p c t -> p (c t)"),
            )

        ident_f32 = keep.tile([P, P], F32)
        make_identity(nc, ident_f32[:])
        ident_bf16 = keep.tile([P, P], BF16)
        make_identity(nc, ident_bf16[:])
        one = keep.tile([P, 1], F32)
        nc.vector.memset(one[:], 1.0)
        warm = keep.tile([P, 1], F32)
        nc.scalar.activation(out=warm[:], in_=one[:], func=ACT.Sqrt)

        x_sb = keep.tile([P, TOKEN_TILES, E], BF16)
        b1_rows = keep.tile([P, P], BF16)
        b1_sb = keep.tile([P, F // P], F32)
        b2_all = keep.tile([P, E], BF16)
        g_all = keep.tile([P, E], BF16)
        b_all = keep.tile([P, E], BF16)
        x_words = keep.tile([P, E_PASSES, TOKENS], U32, align_bytes=64)
        x_scales = keep.tile([P, E_PASSES, TOKENS], U8, align_bytes=64)
        h_words = keep.tile([P, F_PASSES, TOKENS], U32, align_bytes=64)
        h_scales = keep.tile([P, F_PASSES, TOKENS], U8, align_bytes=64)
        w1_raw = {}
        w2_raw = {}

        def weight_chunks(s):
            if s < W1_STEPS:
                return [w1_raw[(s, ep)][:] for ep in range(E_PASSES)]
            eh, pair = divmod(s - W1_STEPS, F_PASSES // 2)
            return [w2_raw[(eh, 2 * pair + a)][:] for a in range(2)]

        def interleave_on_tensor(s):
            rows = weight_chunks(s)[1]
            banks_of[s] = []
            for c in range(0, N_TILE, IL_COLS):
                bank = psum.tile([P, IL_COLS, PACK], BF16, tag="il", bufs=2)
                for n in range(0, IL_COLS, P):
                    nc.tensor.matmul(
                        out=bank[:, n : n + P, :].rearrange("p n t -> p t n"),
                        lhsT=ident_bf16[:],
                        rhs=rows[:, :, c + n : c + n + P],
                        start=True,
                        stop=True,
                    )
                banks_of[s].append(bank)

        def regroup_weights(s):
            vector_cols = W1_VECTOR_COLS if s < W1_STEPS else W2_VECTOR_COLS if s < STEPS - TOKEN_TILES else W2_LATE_VECTOR_COLS
            chunks = weight_chunks(s)
            if s not in IL_STEPS:
                return [regroup(rows, vector_cols) for rows in chunks]
            first = regroup(chunks[0], IL_VECTOR_COLS)
            second = stage.tile([P, N_TILE, PACK], BF16, align_bytes=64, bufs=6, tag="grouped")
            for half, bank in enumerate(banks_of[s]):
                nc.scalar.copy(out=second[:, half * IL_COLS : (half + 1) * IL_COLS, :], in_=bank[:])
            return [first, second]

        banks_of = {}
        grouped_of = {}
        h_acc = {}
        h_rows = {}
        m_acc = {}
        z_of = {}
        late = {}

        def first_matmul(s, words, scales):
            h_acc[s] = []
            for t in range(PACK):
                acc = psum.tile([P, N_TILE], F32, tag="bank")
                for ep in range(E_PASSES):
                    nc.tensor.matmul_mx(
                        out=acc[:],
                        lhsT=words[:, ep, t * P : (t + 1) * P].bitcast(FP8X4),
                        lhsT_scale=scales[:, ep, t * P : (t + 1) * P],
                        rhs=x_words[:, ep, :].bitcast(FP8X4),
                        rhs_scale=x_scales[:, ep, :],
                        start=(ep == 0),
                        stop=(ep == E_PASSES - 1),
                    )
                h_acc[s].append(acc)

        def bias_relu(s):
            h_t = stage.tile([P, PACK, TOKENS], BF16, bufs=3)
            for t in range(PACK):
                col = s * PACK + t
                nc.scalar.activation(
                    out=h_t[:, t, :], in_=h_acc[s][t][:], func=ACT.Relu, bias=b1_sb[:, col : col + 1]
                )
            h_rows[s] = h_t

        def second_matmul(s, words, scales):
            eh, pair = divmod(s - W1_STEPS, F_PASSES // 2)
            for a in range(2):
                fp = 2 * pair + a
                for i in range(TOKEN_TILES):
                    if fp == 0:
                        acc = psum.tile([P, N_TILE], F32, tag="il" if eh == 1 and i >= 2 else "bank", bufs=2 if eh == 1 and i >= 2 else 6)
                        m_acc[(eh, i)] = acc
                    nc.tensor.matmul_mx(
                        out=m_acc[(eh, i)][:],
                        lhsT=h_words[:, fp, i * P : (i + 1) * P].bitcast(FP8X4),
                        lhsT_scale=h_scales[:, fp, i * P : (i + 1) * P],
                        rhs=words[:, a, :].bitcast(FP8X4),
                        rhs_scale=scales[:, a, :],
                        start=(fp == 0),
                        stop=(fp == F_PASSES - 1),
                    )

        def add_bias(eh, i):
            cols = slice(eh * N_TILE, (eh + 1) * N_TILE)
            z = late["pool"].tile([P, N_TILE], F32, bufs=3)
            nc.vector.tensor_tensor(out=z[:], in0=m_acc[(eh, i)][:], in1=b2_all[:, cols], op=ALU.add)
            z_of[(eh, i)] = z

        def relu_residual(eh, i):
            cols = slice(eh * N_TILE, (eh + 1) * N_TILE)
            nc.vector.scalar_tensor_tensor(
                out=late["y"][:, i, cols],
                in0=z_of[(eh, i)][:],
                scalar=0.0,
                in1=x_sb[:, i, cols],
                op0=ALU.max,
                op1=ALU.add,
                accum_out=late["y_sum"][:, i, eh : eh + 1],
            )

        def step(s):
            if s + 1 in IL_STEPS:
                interleave_on_tensor(s + 1)
            if 0 <= s - 1 < W1_STEPS:
                bias_relu(s - 1)
            if s + 1 < STEPS:
                grouped_of[s + 1] = regroup_weights(s + 1)
            if 0 <= s - 2 < W1_STEPS:
                h_grouped = regroup(h_rows[s - 2][:], N_TILE)
            if s >= STEPS - TOKEN_TILES:
                add_bias(0, s - (STEPS - TOKEN_TILES))
            words = stage.tile([P, 2, N_TILE], U32, align_bytes=64)
            scales = stage.tile([P, 2, N_TILE], U8, align_bytes=64)
            for a in range(2):
                quantise(grouped_of[s][a], words[:, a, :], scales[:, a, :])
            if 0 <= s - 2 < W1_STEPS:
                quantise(h_grouped, h_words[:, s - 2, :], h_scales[:, s - 2, :])
            if s < W1_STEPS:
                first_matmul(s, words, scales)
            else:
                second_matmul(s, words, scales)
            if s >= STEPS - TOKEN_TILES:
                relu_residual(0, s - (STEPS - TOKEN_TILES))

        with tc.tile_pool(name="w1", bufs=1) as w1_pool:
            for i in range(TOKEN_TILES):
                nc.sync.dma_start(out=x_sb[:, i, :], in_=x_rows[:, i, :])
            nc.vector.memset(b1_rows[:], 0.0)
            nc.sync.dma_start(out=b1_rows[: F // P, :], in_=mlp_b1.rearrange("(r c) -> r c", c=P))
            for s in range(W1_STEPS):
                for ep in range(E_PASSES):
                    w1_rows = w1_pool.tile([P, PACK, N_TILE], BF16, name="w1_raw%d_%d" % (s, ep))
                    nc.sync.dma_start(
                        out=w1_rows[:],
                        in_=mlp_w1[
                            ep * K_PASS : (ep + 1) * K_PASS, s * N_TILE : (s + 1) * N_TILE
                        ].rearrange("(p j) w -> p j w", j=PACK),
                    )
                    w1_raw[(s, ep)] = w1_rows
            for eh in range(E_HALVES):
                for fp in range(F_PASSES):
                    w2_rows = keep.tile([P, PACK, N_TILE], BF16, name="w2_raw%d_%d" % (eh, fp))
                    nc.sync.dma_start(
                        out=w2_rows[:],
                        in_=mlp_w2[
                            fp * K_PASS : (fp + 1) * K_PASS, eh * N_TILE : (eh + 1) * N_TILE
                        ].rearrange("(t p) e -> p t e", p=P),
                    )
                    w2_raw[(eh, fp)] = w2_rows
            nc.sync.dma_start(out=b2_all[:], in_=mlp_b2.partition_broadcast(P))
            nc.sync.dma_start(out=g_all[:], in_=ln3_g.partition_broadcast(P))
            nc.sync.dma_start(out=b_all[:], in_=ln3_b.partition_broadcast(P))

            x_pairs = x_sb[:].bitcast(F32).rearrange("r i (ep p u) -> r i ep u p", ep=E_PASSES, u=2)
            x_grouped = keep.tile([P, E_PASSES, TOKENS, PACK], BF16, align_bytes=64)
            x_grouped_pairs = x_grouped[:].bitcast(F32)
            for i in range(TOKEN_TILES):
                xt = psum.tile([P, E_PASSES, 2, P], F32, tag="bank")
                for ep in range(E_PASSES):
                    for u in range(2):
                        nc.tensor.transpose(out=xt[:, ep, u, :], in_=x_pairs[:, i, ep, u, :], identity=ident_f32[:])
                dst = x_grouped_pairs[:, :, i * P : (i + 1) * P, :]
                src = xt[:].rearrange("p ep u r -> p ep r u")
                if i % 2 == 0:
                    nc.vector.tensor_copy(out=dst, in_=src)
                else:
                    nc.scalar.copy(out=dst, in_=src)

            b1_t = psum.tile([P, P], BF16, tag="bank")
            nc.tensor.transpose(out=b1_t[:], in_=b1_rows[:], identity=ident_bf16[:])

            grouped_of[0] = regroup_weights(0)
            nc.vector.quantize_mx(
                out=x_words[:].rearrange("p ep c -> p (ep c)").bitcast(FP8X4),
                scales=x_scales[:].rearrange("p ep c -> p (ep c)"),
                in_=x_grouped[:].rearrange("p ep c t -> p (ep c t)"),
            )
            nc.vector.tensor_copy(out=b1_sb[:], in_=b1_t[:, : F // P])

            for s in range(W1_STEPS):
                step(s)

        tail = ctx.enter_context(tc.tile_pool(name="tail", bufs=2))
        late["pool"] = tail
        y = tail.tile([P, TOKEN_TILES, E], F32, bufs=1)
        late["y"] = y
        y_sum = tail.tile([P, TOKEN_TILES, E_HALVES], F32, bufs=1)
        late["y_sum"] = y_sum
        neg_mean = tail.tile([P, TOKEN_TILES], F32, bufs=1)
        sq_sum = tail.tile([P, TOKEN_TILES], F32, bufs=1)
        std = tail.tile([P, TOKEN_TILES], F32, bufs=1)
        rstd = tail.tile([P, TOKEN_TILES], F32, bufs=1)

        for s in range(W1_STEPS, STEPS):
            step(s)

        for i in range(TOKEN_TILES + 2):
            if i < TOKEN_TILES:
                add_bias(1, i)
            if 0 <= i - 1 < TOKEN_TILES:
                relu_residual(1, i - 1)
            if i >= 2:
                j = i - 2
                nc.vector.tensor_scalar(
                    out=neg_mean[:, j : j + 1],
                    in0=y_sum[:, j, 0:1],
                    scalar1=y_sum[:, j, 1:2],
                    scalar2=-1.0 / E,
                    op0=ALU.add,
                    op1=ALU.mult,
                )
                squares = tail.tile([P, E], BF16)
                nc.scalar.activation(
                    out=squares[:],
                    in_=y[:, j, :],
                    func=ACT.Square,
                    bias=neg_mean[:, j : j + 1],
                    accum_out=sq_sum[:, j : j + 1],
                )
        nc.scalar.activation(out=std[:], in_=sq_sum[:], func=ACT.Sqrt, scale=1.0 / E, bias=EPS)
        normed = []
        for i in range(TOKEN_TILES):
            if i == TOKEN_TILES - 1:
                nc.vector.reciprocal(out=rstd[:], in_=std[:])
            centred = tail.tile([P, E], F32, bufs=TOKEN_TILES)
            nc.vector.scalar_tensor_tensor(
                out=centred[:],
                in0=y[:, i, :],
                scalar=neg_mean[:, i : i + 1],
                in1=g_all[:],
                op0=ALU.add,
                op1=ALU.mult,
            )
            normed.append(centred)
        for i in range(TOKEN_TILES):
            nc.vector.scalar_tensor_tensor(
                out=normed[i][:],
                in0=normed[i][:],
                scalar=rstd[:, i : i + 1],
                in1=b_all[:],
                op0=ALU.mult,
                op1=ALU.add,
            )
            nc.sync.dma_start(out=out_rows[:, i, :], in_=normed[i][:])
